import numpy as np
import ml_dtypes


def mxq(x, axis, fmt="e4m3"):
    dtype, down = {"e4m3": (ml_dtypes.float8_e4m3fn, 7), "e5m2": (ml_dtypes.float8_e5m2, 14)}[fmt]
    v = np.moveaxis(np.asarray(x, np.float32).astype(ml_dtypes.bfloat16).astype(np.float64), axis, -1)
    blocks = v.reshape(v.shape[:-1] + (-1, 32))
    amax = np.abs(blocks).max(-1, keepdims=True)
    byte = np.maximum(np.where(amax > 0, np.frexp(amax)[1] - 1 + 127, 0) - down, 1)
    scale = np.exp2(byte - 127.0)
    codes = (blocks / scale).astype(np.float32).astype(dtype).astype(np.float64)
    return np.moveaxis((codes * scale).reshape(v.shape), -1, axis)


WIDE = False


def mx_kscale(k):
    if not WIDE:
        return np.ones(k)
    levels = np.array([10, -10, 5, -5, 0])
    a = np.random.permutation(np.resize(levels, k // 512 * 4)).reshape(k // 512, 4)
    idx = np.arange(k)
    return np.exp2(a[idx // 512, idx % 128 // 32])


BF16 = ml_dtypes.bfloat16


def bf(x):
    return np.asarray(x, np.float32).astype(BF16)


def f64(x):
    return np.asarray(x).astype(np.float64)


B, M, N, P = 6, 1024, 1024, 512
EPS = 1e-05


def normalize(v, axes, gamma, beta):
    mean = v.mean(axis=axes, keepdims=True)
    std = np.sqrt(v.var(axis=axes, keepdims=True, ddof=1))
    return gamma * ((v - mean) / (std + EPS)) + beta


def setup_inputs():
    s = mx_kscale(M)
    return {"x": bf(np.random.standard_normal((B, M, N)) * s[:, None]),
            "permuted_xj_y": bf(np.random.standard_normal((M, P)) * 0.5 / np.sqrt(M) / s[:, None]),
            "permuted_xi_y": bf(np.random.standard_normal((N, P)) * 2.0 / np.sqrt(N)),
            "gamma_p_sum": bf(1.0 + 0.1 * np.random.standard_normal(P)),
            "gamma_p": bf(1.0 + 0.1 * np.random.standard_normal((P, P))),
            "beta_p_sum": bf(0.1 * np.random.standard_normal(P)),
            "beta_p": bf(0.1 * np.random.standard_normal((P, P)))}


def reference(x, permuted_xj_y, permuted_xi_y, gamma_p_sum, gamma_p, beta_p_sum, beta_p):
    permuted = np.swapaxes(f64(x), -1, -2)
    pyy = mxq(permuted, 2, "e4m3") @ mxq(f64(permuted_xj_y), 0, "e4m3")
    p_sum = normalize(pyy.sum(axis=-2), (-1,), f64(gamma_p_sum), f64(beta_p_sum)) + 1.0
    pyy = mxq(np.swapaxes(pyy, -1, -2), 2, "e4m3") @ mxq(f64(permuted_xi_y), 0, "e4m3")
    pyy = np.swapaxes(pyy, -1, -2)
    pyy = normalize(pyy, (-2, -1), f64(gamma_p), f64(beta_p))
    return pyy, p_sum

@@ -1,0 +1,307 @@
+from contextlib import ExitStack
+
+import concourse.mybir as mybir
+from concourse.masks import make_identity
+
+F32 = mybir.dt.float32
+BF16 = mybir.dt.bfloat16
+U32 = mybir.dt.uint32
+U8 = mybir.dt.uint8
+FP8X4 = mybir.dt.float8_e4m3fn_x4
+ALU = mybir.AluOpType
+ACT = mybir.ActivationFunctionType
+AXIS = mybir.AxisListType
+
+B = 6
+M = 1024
+N = 1024
+J = 512
+EPS = 1e-05
+
+P = 128
+PACK = 4
+K_PASS = P * PACK
+PASSES = M // K_PASS
+J_TILES = J // P
+RUN = 4
+
+UNIT_ROUNDS = J_TILES
+ROUNDS = PASSES * UNIT_ROUNDS
+PIECES = 2 * PASSES
+HEAD_PIECE_COLS = 80
+PIECE_COLS = 192
+AHEAD = UNIT_ROUNDS + 2
+
+FLOPS = B * (2 * M * N * J + 2 * N * J * J)
+
+
+def tile_selfprojection_pb_kernel(
+    tc, x, permuted_xj_y, permuted_xi_y, gamma_p_sum, gamma_p, beta_p_sum, beta_p, out_0, out_1
+):
+    nc = tc.nc
+    with ExitStack() as pools:
+        const = pools.enter_context(tc.tile_pool(name="const", bufs=1))
+        raw_pool = pools.enter_context(tc.tile_pool(name="raw", bufs=4))
+        grouped_pool = pools.enter_context(tc.tile_pool(name="grouped", bufs=3))
+        x_pool = pools.enter_context(tc.tile_pool(name="x_quantised", bufs=4))
+        y_pool = pools.enter_context(tc.tile_pool(name="y_quantised", bufs=2))
+        result = pools.enter_context(tc.tile_pool(name="result", bufs=2))
+        stats = pools.enter_context(tc.tile_pool(name="stats", bufs=2))
+        psum = pools.enter_context(tc.psum_pool(name="psum", bufs=1))
+
+        one = const.tile([P, 1], F32)
+        nc.vector.memset(one[:], 1.0)
+        warm = const.tile([P, 1], F32)
+        nc.scalar.activation(out=warm[:], in_=one[:], func=ACT.Sqrt)
+
+        identity = const.tile([P, P], F32)
+        make_identity(nc, identity[:])
+        pick = const.tile([P, 2 * P], F32)
+        nc.vector.memset(pick[:], 0.0)
+        nc.vector.memset(pick[:, P : P + 1], 1.0)
+
+        def load_unit(view):
+            raw = raw_pool.tile([P, PASSES, PACK, J], BF16, name="raw")
+            for c in range(PASSES):
+                nc.sync.dma_start(out=raw[:, c], in_=view[:, c])
+            grouped = grouped_pool.tile([P, PASSES, J, PACK], BF16, name="grouped", align_bytes=64)
+            return raw, grouped
+
+        def scalar_regroups_piece(raw, grouped, i, width):
+            c, half = divmod(i, 2)
+            cols = slice(half * width, (half + 1) * width)
+            nc.scalar.copy(
+                out=grouped[:, c, cols, :].rearrange("p (k i) t -> p k t i", i=RUN),
+                in_=raw[:, c, :, cols].rearrange("p t (k i) -> p k t i", i=RUN),
+            )
+
+        def vector_regroups_rest(raw, grouped, width):
+            nc.vector.tensor_copy(
+                out=grouped[:, :, 2 * width :, :].rearrange("p c (k i) t -> p c k t i", i=RUN),
+                in_=raw[:, :, :, 2 * width :].rearrange("p c t (k i) -> p c k t i", i=RUN),
+            )
+
+        def quantise_unit(grouped, pool, name):
+            words = pool.tile([P, PASSES, J], U32, name=name + "_words", align_bytes=64)
+            scales = pool.tile([P, PASSES, J], U8, name=name + "_scales", align_bytes=64)
+            nc.vector.quantize_mx(
+                out=words[:].rearrange("p c w -> p (c w)").bitcast(FP8X4),
+                scales=scales[:].rearrange("p c w -> p (c w)"),
+                in_=grouped[:].rearrange("p c w t -> p (c w t)"),
+            )
+            return words, scales
+
+        def quantise_weight(view, name, width):
+            raw, grouped = load_unit(view)
+            vector_regroups_rest(raw, grouped, width)
+            for i in range(PIECES):
+                scalar_regroups_piece(raw, grouped, i, width)
+            return quantise_unit(grouped, const, name)
+
+        x_tiles = {}
+        x_words = {}
+
+        def prepare_x(step):
+            u, i = divmod(step, PIECES)
+            width = HEAD_PIECE_COLS if u == 0 else PIECE_COLS
+            if i == 0:
+                if u < B * PASSES:
+                    b, g = divmod(u, PASSES)
+                    columns = x[b, :, g * J : (g + 1) * J]
+                    x_tiles[u] = load_unit(
+                        columns.rearrange("(c p t) n -> p c t n", c=PASSES, t=PACK)
+                    )
+                    vector_regroups_rest(x_tiles[u][0], x_tiles[u][1], width)
+                if u > 0:
+                    x_words[u - 1] = quantise_unit(x_tiles[u - 1][1], x_pool, "x")
+            if u < B * PASSES:
+                scalar_regroups_piece(x_tiles[u][0], x_tiles[u][1], i, width)
+
+        y_grouped = {}
+        y_words = {}
+        y_scales = {}
+        column_sum = {}
+
+        def first_contraction_round(b, r):
+            g, jt = divmod(r, UNIT_ROUNDS)
+            words, scales = x_words[b * PASSES + g]
+            if r == 0:
+                y_grouped[b] = y_pool.tile(
+                    [P, PASSES, J, PACK], BF16, name="y_grouped", align_bytes=64
+                )
+                y_words[b] = y_pool.tile([P, PASSES, J], U32, name="y_words", align_bytes=64)
+                y_scales[b] = y_pool.tile([P, PASSES, J], U8, name="y_scales", align_bytes=64)
+                column_sum[b] = psum.tile([P, J], F32, name="column_sum")
+
+            rows = slice(jt * P, (jt + 1) * P)
+            for c in range(PASSES):
+                nc.tensor.matmul_mx(
+                    out=column_sum[b][:],
+                    lhsT=words[:, c, rows].bitcast(FP8X4),
+                    lhsT_scale=scales[:, c, rows],
+                    rhs=wj_words[:, c, :].bitcast(FP8X4),
+                    rhs_scale=wj_scales[:, c, :],
+                    start=(r == 0 and c == 0),
+                    stop=(r == ROUNDS - 1 and c == PASSES - 1),
+                )
+
+            y_bank = psum.tile([P, PACK, P], F32, name="y_bank", tag="work", bufs=3)
+            cols = slice(jt * P, (jt + 1) * P)
+            for t in range(PACK):
+                rows = slice(t * P, (t + 1) * P)
+                for c in range(PASSES):
+                    nc.tensor.matmul_mx(
+                        out=y_bank[:, t, :],
+                        lhsT=words[:, c, rows].bitcast(FP8X4),
+                        lhsT_scale=scales[:, c, rows],
+                        rhs=wj_words[:, c, cols].bitcast(FP8X4),
+                        rhs_scale=wj_scales[:, c, cols],
+                        start=(c == 0),
+                        stop=(c == PASSES - 1),
+                    )
+            nc.scalar.copy(
+                out=y_grouped[b][:, g, cols, :], in_=y_bank[:].rearrange("p t j -> p j t")
+            )
+            if jt == J_TILES - 1:
+                nc.vector.quantize_mx(
+                    out=y_words[b][:, g, :].bitcast(FP8X4),
+                    scales=y_scales[b][:, g, :],
+                    in_=y_grouped[b][:, g].rearrange("p j t -> p (j t)"),
+                )
+
+        c_rows = const.tile([P, J], F32)
+
+        def add_column_sum(b):
+            partial = stats.tile([P, J], F32, name="partial")
+            nc.scalar.copy(out=partial[:], in_=column_sum[b][:])
+            row = psum.tile([P, J], F32, name="row", tag="work", bufs=3)
+            nc.tensor.matmul(
+                out=row[:], lhsT=pick[:, P - b : 2 * P - b], rhs=partial[:], start=True, stop=True
+            )
+            if b == 0:
+                nc.vector.tensor_copy(out=c_rows[:], in_=row[:])
+            else:
+                nc.vector.tensor_tensor(out=c_rows[:], in0=row[:], in1=c_rows[:], op=ALU.add)
+
+        def std_of(population_var, count, rows):
+            std = stats.tile([P, 1], F32, name="std")
+            nc.scalar.activation(
+                out=std[:rows], in_=population_var, func=ACT.Sqrt, scale=count / (count - 1.0)
+            )
+            return std
+
+        def inverse_of(std, rows):
+            padded = stats.tile([P, 1], F32, name="padded")
+            nc.vector.tensor_scalar_add(out=padded[:rows], in0=std[:rows], scalar1=EPS)
+            inverse = stats.tile([P, 1], F32, name="inverse")
+            nc.vector.reciprocal(out=inverse[:rows], in_=padded[:rows])
+            return inverse
+
+        def write_p_sum():
+            bias_plus_one = const.tile([B, J], F32)
+            nc.vector.tensor_scalar_add(out=bias_plus_one[:], in0=bias_rows[:], scalar1=1.0)
+            six = stats.tile([P, 6], F32, name="c_six")
+            nc.vector.bn_stats(out=six[:B], in_=c_rows[:B, :])
+            mean_var = stats.tile([P, 2], F32, name="c_mean_var")
+            nc.vector.bn_aggr(out=mean_var[:B], in_=six[:B])
+            std = std_of(mean_var[:B, 1:2], J, B)
+            c_centred = const.tile([B, J], F32)
+            nc.vector.scalar_tensor_tensor(
+                out=c_centred[:], in0=c_rows[:B, :], scalar=mean_var[:B, 0:1], in1=gain_rows[:],
+                op0=ALU.subtract, op1=ALU.mult,
+            )
+            inverse = inverse_of(std, B)
+            p_sum = const.tile([B, J], F32)
+            nc.vector.scalar_tensor_tensor(
+                out=p_sum[:], in0=c_centred[:], scalar=inverse[:B, 0:1], in1=bias_plus_one[:],
+                op0=ALU.mult, op1=ALU.add,
+            )
+            nc.sync.dma_start(out=out_1, in_=p_sum[:])
+
+        def second_contraction(b):
+            z_banks = []
+            six = stats.tile([P, J_TILES, 6], F32, name="z_six")
+            for it in range(J_TILES):
+                z_bank = psum.tile([P, J], F32, name="z_bank", bufs=J_TILES)
+                z_banks.append(z_bank)
+                cols = slice(it * P, (it + 1) * P)
+                for g in range(PASSES):
+                    nc.tensor.matmul_mx(
+                        out=z_bank[:],
+                        lhsT=wi_words[:, g, cols].bitcast(FP8X4),
+                        lhsT_scale=wi_scales[:, g, cols],
+                        rhs=y_words[b][:, g, :].bitcast(FP8X4),
+                        rhs_scale=y_scales[b][:, g, :],
+                        start=(g == 0),
+                        stop=(g == PASSES - 1),
+                    )
+                nc.vector.bn_stats(out=six[:, it, :], in_=z_bank[:])
+            mean_var = stats.tile([P, 2], F32, name="z_mean_var")
+            nc.vector.bn_aggr(out=mean_var[:], in_=six[:].rearrange("p a s -> p (a s)"))
+            spread = psum.tile([P, 2, P], F32, name="spread", tag="work", bufs=3)
+            for s in range(2):
+                nc.tensor.matmul(
+                    out=spread[:, s, :],
+                    lhsT=mean_var[:, s : s + 1].to_broadcast([P, P]),
+                    rhs=identity[:],
+                    start=True,
+                    stop=True,
+                )
+            means_six = stats.tile([P, 6], F32, name="means_six")
+            nc.vector.bn_stats(out=means_six[:], in_=spread[:, 0, :])
+            whole = stats.tile([P, 2], F32, name="whole")
+            nc.vector.bn_aggr(out=whole[:], in_=means_six[:])
+            var_sum = stats.tile([P, 1], F32, name="var_sum")
+            nc.vector.reduce_sum(out=var_sum[:], in_=spread[:, 1, :], axis=AXIS.X)
+            population_var = stats.tile([P, 1], F32, name="population_var")
+            nc.vector.tensor_scalar(
+                out=population_var[:], in0=var_sum[:], scalar1=1.0 / P, scalar2=whole[:, 1:2],
+                op0=ALU.mult, op1=ALU.add,
+            )
+            std = std_of(population_var[:], J * J, P)
+
+            centred = result.tile([P, J_TILES, J], F32, name="centred")
+            for it in range(J_TILES):
+                nc.vector.scalar_tensor_tensor(
+                    out=centred[:, it, :], in0=z_banks[it][:], scalar=whole[:, 0:1],
+                    in1=gain[:, it, :], op0=ALU.subtract, op1=ALU.mult,
+                )
+            inverse = inverse_of(std, P)
+            normal = result.tile([P, J_TILES, J], F32, name="normal")
+            for it in range(J_TILES):
+                nc.vector.scalar_tensor_tensor(
+                    out=normal[:, it, :], in0=centred[:, it, :], scalar=inverse[:, 0:1],
+                    in1=bias[:, it, :], op0=ALU.mult, op1=ALU.add,
+                )
+                nc.sync.dma_start(out=out_0[b, it * P : (it + 1) * P, :], in_=normal[:, it, :])
+
+        for step in range(PIECES):
+            prepare_x(step)
+        wj_words, wj_scales = quantise_weight(
+            permuted_xj_y.rearrange("(c p t) j -> p c t j", c=PASSES, t=PACK), "wj", HEAD_PIECE_COLS
+        )
+        for step in range(PIECES, AHEAD):
+            prepare_x(step)
+        wi_words, wi_scales = quantise_weight(
+            permuted_xi_y.rearrange("(g t p) i -> p g t i", g=PASSES, t=PACK), "wi", PIECE_COLS
+        )
+        gain = const.tile([P, J_TILES, J], BF16)
+        nc.sync.dma_start(out=gain[:], in_=gamma_p.rearrange("(a p) j -> p a j", p=P))
+        bias = const.tile([P, J_TILES, J], BF16)
+        nc.sync.dma_start(out=bias[:], in_=beta_p.rearrange("(a p) j -> p a j", p=P))
+        gain_rows = const.tile([B, J], BF16)
+        nc.sync.dma_start(out=gain_rows[:], in_=gamma_p_sum.partition_broadcast(B))
+        bias_rows = const.tile([B, J], BF16)
+        nc.sync.dma_start(out=bias_rows[:], in_=beta_p_sum.partition_broadcast(B))
+
+        for b in range(B):
+            for r in range(ROUNDS):
+                step = b * ROUNDS + r + AHEAD
+                if step <= B * ROUNDS:
+                    prepare_x(step)
+                first_contraction_round(b, r)
+                if b > 0 and r == 1:
+                    second_contraction(b - 1)
+            add_column_sum(b)
+        write_p_sum()
+        second_contraction(B - 1)

@@ -25,12 +25,17 @@ PASSES = M // K_PASS
 J_TILES = J // P
 RUN = 4
 
+UNITS = B * PASSES
 UNIT_ROUNDS = J_TILES
 ROUNDS = PASSES * UNIT_ROUNDS
 PIECES = 2 * PASSES
-HEAD_PIECE_COLS = 80
-PIECE_COLS = 192
-AHEAD = UNIT_ROUNDS + 2
+FIRST_PIECE_COLS = 128
+EARLY_PIECE_COLS = 80
+PIECE_COLS = 256
+EARLY_UNITS = 2 * PASSES
+AHEAD = UNIT_ROUNDS + 3
+LOAD_AHEAD = 2
+WI_ROUND = 3
 
 FLOPS = B * (2 * M * N * J + 2 * N * J * J)
 
@@ -39,15 +44,16 @@ def tile_selfprojection_pb_kernel(
     tc, x, permuted_xj_y, permuted_xi_y, gamma_p_sum, gamma_p, beta_p_sum, beta_p, out_0, out_1
 ):
     nc = tc.nc
-    with ExitStack() as pools:
-        const = pools.enter_context(tc.tile_pool(name="const", bufs=1))
-        raw_pool = pools.enter_context(tc.tile_pool(name="raw", bufs=4))
-        grouped_pool = pools.enter_context(tc.tile_pool(name="grouped", bufs=3))
-        x_pool = pools.enter_context(tc.tile_pool(name="x_quantised", bufs=4))
-        y_pool = pools.enter_context(tc.tile_pool(name="y_quantised", bufs=2))
-        result = pools.enter_context(tc.tile_pool(name="result", bufs=2))
-        stats = pools.enter_context(tc.tile_pool(name="stats", bufs=2))
-        psum = pools.enter_context(tc.psum_pool(name="psum", bufs=1))
+    with ExitStack() as stack:
+        const = stack.enter_context(tc.tile_pool(name="const", bufs=1))
+        raw_pool = stack.enter_context(tc.tile_pool(name="raw", bufs=4))
+        grouped_pool = stack.enter_context(tc.tile_pool(name="grouped", bufs=3))
+        x_pool = stack.enter_context(tc.tile_pool(name="x_quantised", bufs=4))
+        y_pool = stack.enter_context(tc.tile_pool(name="y_quantised", bufs=2))
+        result = stack.enter_context(tc.tile_pool(name="result", bufs=2))
+        stats = stack.enter_context(tc.tile_pool(name="stats", bufs=2))
+        partials = stack.enter_context(tc.tile_pool(name="partials", bufs=B))
+        psum = stack.enter_context(tc.psum_pool(name="psum", bufs=1))
 
         one = const.tile([P, 1], F32)
         nc.vector.memset(one[:], 1.0)
@@ -64,8 +70,20 @@ def tile_selfprojection_pb_kernel(
             raw = raw_pool.tile([P, PASSES, PACK, J], BF16, name="raw")
             for c in range(PASSES):
                 nc.sync.dma_start(out=raw[:, c], in_=view[:, c])
-            grouped = grouped_pool.tile([P, PASSES, J, PACK], BF16, name="grouped", align_bytes=64)
-            return raw, grouped
+            return raw
+
+        def x_view(u):
+            b, g = divmod(u, PASSES)
+            return x[b, :, g * J : (g + 1) * J].rearrange("(c p t) n -> p c t n", c=PASSES, t=PACK)
+
+        def new_grouped():
+            return grouped_pool.tile([P, PASSES, J, PACK], BF16, name="grouped", align_bytes=64)
+
+        def vector_regroups_rest(raw, grouped, width):
+            nc.vector.tensor_copy(
+                out=grouped[:, :, 2 * width :, :].rearrange("p c (k i) t -> p c k t i", i=RUN),
+                in_=raw[:, :, :, 2 * width :].rearrange("p c t (k i) -> p c k t i", i=RUN),
+            )
 
         def scalar_regroups_piece(raw, grouped, i, width):
             c, half = divmod(i, 2)
@@ -73,12 +91,6 @@ def tile_selfprojection_pb_kernel(
             nc.scalar.copy(
                 out=grouped[:, c, cols, :].rearrange("p (k i) t -> p k t i", i=RUN),
                 in_=raw[:, c, :, cols].rearrange("p t (k i) -> p k t i", i=RUN),
-            )
-
-        def vector_regroups_rest(raw, grouped, width):
-            nc.vector.tensor_copy(
-                out=grouped[:, :, 2 * width :, :].rearrange("p c (k i) t -> p c k t i", i=RUN),
-                in_=raw[:, :, :, 2 * width :].rearrange("p c t (k i) -> p c k t i", i=RUN),
             )
 
         def quantise_unit(grouped, pool, name):
@@ -91,36 +103,51 @@ def tile_selfprojection_pb_kernel(
             )
             return words, scales
 
-        def quantise_weight(view, name, width):
-            raw, grouped = load_unit(view)
-            vector_regroups_rest(raw, grouped, width)
-            for i in range(PIECES):
-                scalar_regroups_piece(raw, grouped, i, width)
-            return quantise_unit(grouped, const, name)
+        def prepare_unit_by_passes(raw, pool, name):
+            grouped = new_grouped()
+            words = pool.tile([P, PASSES, J], U32, name=name + "_words", align_bytes=64)
+            scales = pool.tile([P, PASSES, J], U8, name=name + "_scales", align_bytes=64)
+            for c in range(PASSES):
+                nc.vector.tensor_copy(
+                    out=grouped[:, c, 2 * FIRST_PIECE_COLS :, :].rearrange(
+                        "p (k i) t -> p k t i", i=RUN
+                    ),
+                    in_=raw[:, c, :, 2 * FIRST_PIECE_COLS :].rearrange(
+                        "p t (k i) -> p k t i", i=RUN
+                    ),
+                )
+                for i in range(2 * c, 2 * c + 2):
+                    scalar_regroups_piece(raw, grouped, i, FIRST_PIECE_COLS)
+                nc.vector.quantize_mx(
+                    out=words[:, c, :].bitcast(FP8X4),
+                    scales=scales[:, c, :],
+                    in_=grouped[:, c].rearrange("p w t -> p (w t)"),
+                )
+            return words, scales
 
-        x_tiles = {}
+        x_raw = {}
+        x_grouped = {}
         x_words = {}
 
         def prepare_x(step):
             u, i = divmod(step, PIECES)
-            width = HEAD_PIECE_COLS if u == 0 else PIECE_COLS
-            if i == 0:
-                if u < B * PASSES:
-                    b, g = divmod(u, PASSES)
-                    columns = x[b, :, g * J : (g + 1) * J]
-                    x_tiles[u] = load_unit(
-                        columns.rearrange("(c p t) n -> p c t n", c=PASSES, t=PACK)
-                    )
-                    vector_regroups_rest(x_tiles[u][0], x_tiles[u][1], width)
-                if u > 0:
-                    x_words[u - 1] = quantise_unit(x_tiles[u - 1][1], x_pool, "x")
-            if u < B * PASSES:
-                scalar_regroups_piece(x_tiles[u][0], x_tiles[u][1], i, width)
+            width = EARLY_PIECE_COLS if u < EARLY_UNITS else PIECE_COLS
+            if i == 0 and u + LOAD_AHEAD < UNITS:
+                x_raw[u + LOAD_AHEAD] = load_unit(x_view(u + LOAD_AHEAD))
+            if i == 0 and u < UNITS:
+                x_grouped[u] = new_grouped()
+                if u < EARLY_UNITS:
+                    vector_regroups_rest(x_raw[u], x_grouped[u], width)
+            if i == 1 and u - 1 not in x_words:
+                x_words[u - 1] = quantise_unit(x_grouped[u - 1], x_pool, "x")
+            if u < UNITS:
+                scalar_regroups_piece(x_raw[u], x_grouped[u], i, width)
 
         y_grouped = {}
         y_words = {}
         y_scales = {}
         column_sum = {}
+        partial = {}
 
         def first_contraction_round(b, r):
             g, jt = divmod(r, UNIT_ROUNDS)
@@ -144,6 +171,9 @@ def tile_selfprojection_pb_kernel(
                     start=(r == 0 and c == 0),
                     stop=(r == ROUNDS - 1 and c == PASSES - 1),
                 )
+            if r == ROUNDS - 1:
+                partial[b] = partials.tile([P, J], F32, name="partial")
+                nc.scalar.copy(out=partial[b][:], in_=column_sum[b][:])
 
             y_bank = psum.tile([P, PACK, P], F32, name="y_bank", tag="work", bufs=3)
             cols = slice(jt * P, (jt + 1) * P)
@@ -162,26 +192,23 @@ def tile_selfprojection_pb_kernel(
             nc.scalar.copy(
                 out=y_grouped[b][:, g, cols, :], in_=y_bank[:].rearrange("p t j -> p j t")
             )
-            if jt == J_TILES - 1:
-                nc.vector.quantize_mx(
-                    out=y_words[b][:, g, :].bitcast(FP8X4),
-                    scales=y_scales[b][:, g, :],
-                    in_=y_grouped[b][:, g].rearrange("p j t -> p (j t)"),
-                )
 
-        c_rows = const.tile([P, J], F32)
+        def quantise_y(b, g):
+            nc.vector.quantize_mx(
+                out=y_words[b][:, g, :].bitcast(FP8X4),
+                scales=y_scales[b][:, g, :],
+                in_=y_grouped[b][:, g].rearrange("p j t -> p (j t)"),
+            )
+
+        c_rows = {}
 
         def add_column_sum(b):
-            partial = stats.tile([P, J], F32, name="partial")
-            nc.scalar.copy(out=partial[:], in_=column_sum[b][:])
-            row = psum.tile([P, J], F32, name="row", tag="work", bufs=3)
-            nc.tensor.matmul(
-                out=row[:], lhsT=pick[:, P - b : 2 * P - b], rhs=partial[:], start=True, stop=True
-            )
             if b == 0:
-                nc.vector.tensor_copy(out=c_rows[:], in_=row[:])
-            else:
-                nc.vector.tensor_tensor(out=c_rows[:], in0=row[:], in1=c_rows[:], op=ALU.add)
+                c_rows[0] = psum.tile([P, J], F32, name="c_bank", tag="work", bufs=3)
+            nc.tensor.matmul(
+                out=c_rows[0][:], lhsT=pick[:, P - b : 2 * P - b], rhs=partial[b][:],
+                start=(b == 0), stop=(b == B - 1),
+            )
 
         def std_of(population_var, count, rows):
             std = stats.tile([P, 1], F32, name="std")
@@ -197,20 +224,22 @@ def tile_selfprojection_pb_kernel(
             nc.vector.reciprocal(out=inverse[:rows], in_=padded[:rows])
             return inverse
 
-        def write_p_sum():
-            bias_plus_one = const.tile([B, J], F32)
-            nc.vector.tensor_scalar_add(out=bias_plus_one[:], in0=bias_rows[:], scalar1=1.0)
+        c_centred = const.tile([B, J], F32)
+        c_std = {}
+
+        def centre_c():
             six = stats.tile([P, 6], F32, name="c_six")
-            nc.vector.bn_stats(out=six[:B], in_=c_rows[:B, :])
+            nc.vector.bn_stats(out=six[:B], in_=c_rows[0][:B, :])
             mean_var = stats.tile([P, 2], F32, name="c_mean_var")
             nc.vector.bn_aggr(out=mean_var[:B], in_=six[:B])
-            std = std_of(mean_var[:B, 1:2], J, B)
-            c_centred = const.tile([B, J], F32)
+            c_std[0] = std_of(mean_var[:B, 1:2], J, B)
             nc.vector.scalar_tensor_tensor(
-                out=c_centred[:], in0=c_rows[:B, :], scalar=mean_var[:B, 0:1], in1=gain_rows[:],
+                out=c_centred[:], in0=c_rows[0][:B, :], scalar=mean_var[:B, 0:1], in1=gain_rows[:],
                 op0=ALU.subtract, op1=ALU.mult,
             )
-            inverse = inverse_of(std, B)
+
+        def write_p_sum():
+            inverse = inverse_of(c_std[0], B)
             p_sum = const.tile([B, J], F32)
             nc.vector.scalar_tensor_tensor(
                 out=p_sum[:], in0=c_centred[:], scalar=inverse[:B, 0:1], in1=bias_plus_one[:],
@@ -218,16 +247,22 @@ def tile_selfprojection_pb_kernel(
             )
             nc.sync.dma_start(out=out_1, in_=p_sum[:])
 
+        z_banks = {}
+        z_mean_var = {}
+        z_whole = {}
+        z_std = {}
+        z_inverse = {}
+        centred = {}
+        normal = {}
+
         def second_contraction(b):
-            z_banks = []
             six = stats.tile([P, J_TILES, 6], F32, name="z_six")
             for it in range(J_TILES):
-                z_bank = psum.tile([P, J], F32, name="z_bank", bufs=J_TILES)
-                z_banks.append(z_bank)
+                z_banks[b, it] = psum.tile([P, J], F32, name="z_bank", bufs=J_TILES)
                 cols = slice(it * P, (it + 1) * P)
                 for g in range(PASSES):
                     nc.tensor.matmul_mx(
-                        out=z_bank[:],
+                        out=z_banks[b, it][:],
                         lhsT=wi_words[:, g, cols].bitcast(FP8X4),
                         lhsT_scale=wi_scales[:, g, cols],
                         rhs=y_words[b][:, g, :].bitcast(FP8X4),
@@ -235,73 +270,106 @@ def tile_selfprojection_pb_kernel(
                         start=(g == 0),
                         stop=(g == PASSES - 1),
                     )
-                nc.vector.bn_stats(out=six[:, it, :], in_=z_bank[:])
-            mean_var = stats.tile([P, 2], F32, name="z_mean_var")
-            nc.vector.bn_aggr(out=mean_var[:], in_=six[:].rearrange("p a s -> p (a s)"))
+                nc.vector.bn_stats(out=six[:, it, :], in_=z_banks[b, it][:])
+            z_mean_var[b] = stats.tile([P, 2], F32, name="z_mean_var")
+            nc.vector.bn_aggr(out=z_mean_var[b][:], in_=six[:].rearrange("p a s -> p (a s)"))
+
+        def whole_statistics(b):
             spread = psum.tile([P, 2, P], F32, name="spread", tag="work", bufs=3)
             for s in range(2):
                 nc.tensor.matmul(
                     out=spread[:, s, :],
-                    lhsT=mean_var[:, s : s + 1].to_broadcast([P, P]),
+                    lhsT=z_mean_var[b][:, s : s + 1].to_broadcast([P, P]),
                     rhs=identity[:],
                     start=True,
                     stop=True,
                 )
             means_six = stats.tile([P, 6], F32, name="means_six")
             nc.vector.bn_stats(out=means_six[:], in_=spread[:, 0, :])
-            whole = stats.tile([P, 2], F32, name="whole")
-            nc.vector.bn_aggr(out=whole[:], in_=means_six[:])
+            z_whole[b] = stats.tile([P, 2], F32, name="whole")
+            nc.vector.bn_aggr(out=z_whole[b][:], in_=means_six[:])
             var_sum = stats.tile([P, 1], F32, name="var_sum")
             nc.vector.reduce_sum(out=var_sum[:], in_=spread[:, 1, :], axis=AXIS.X)
             population_var = stats.tile([P, 1], F32, name="population_var")
             nc.vector.tensor_scalar(
-                out=population_var[:], in0=var_sum[:], scalar1=1.0 / P, scalar2=whole[:, 1:2],
-                op0=ALU.mult, op1=ALU.add,
+                out=population_var[:], in0=var_sum[:], scalar1=1.0 / P,
+                scalar2=z_whole[b][:, 1:2], op0=ALU.mult, op1=ALU.add,
             )
-            std = std_of(population_var[:], J * J, P)
+            z_std[b] = std_of(population_var[:], J * J, P)
 
-            centred = result.tile([P, J_TILES, J], F32, name="centred")
+        def centre_z(b):
+            centred[b] = result.tile([P, J_TILES, J], F32, name="centred")
             for it in range(J_TILES):
                 nc.vector.scalar_tensor_tensor(
-                    out=centred[:, it, :], in0=z_banks[it][:], scalar=whole[:, 0:1],
+                    out=centred[b][:, it, :], in0=z_banks[b, it][:], scalar=z_whole[b][:, 0:1],
                     in1=gain[:, it, :], op0=ALU.subtract, op1=ALU.mult,
                 )
-            inverse = inverse_of(std, P)
-            normal = result.tile([P, J_TILES, J], F32, name="normal")
-            for it in range(J_TILES):
-                nc.vector.scalar_tensor_tensor(
-                    out=normal[:, it, :], in0=centred[:, it, :], scalar=inverse[:, 0:1],
-                    in1=bias[:, it, :], op0=ALU.mult, op1=ALU.add,
-                )
-                nc.sync.dma_start(out=out_0[b, it * P : (it + 1) * P, :], in_=normal[:, it, :])
+            z_inverse[b] = inverse_of(z_std[b], P)
+            normal[b] = result.tile([P, J_TILES, J], F32, name="normal")
 
-        for step in range(PIECES):
-            prepare_x(step)
-        wj_words, wj_scales = quantise_weight(
-            permuted_xj_y.rearrange("(c p t) j -> p c t j", c=PASSES, t=PACK), "wj", HEAD_PIECE_COLS
-        )
+        def write_out(b, it):
+            nc.vector.scalar_tensor_tensor(
+                out=normal[b][:, it, :], in0=centred[b][:, it, :], scalar=z_inverse[b][:, 0:1],
+                in1=bias[:, it, :], op0=ALU.mult, op1=ALU.add,
+            )
+            nc.sync.dma_start(out=out_0[b, it * P : (it + 1) * P, :], in_=normal[b][:, it, :])
+
+        def finish_item(b, r):
+            if r == 0 and b == 0:
+                nc.vector.tensor_scalar_add(out=bias_plus_one[:], in0=bias_rows[:], scalar1=1.0)
+            if r == 0 and b == B - 1:
+                add_column_sum(b)
+            if r == 1:
+                second_contraction(b)
+                if b == B - 1:
+                    centre_c()
+            if r == 2:
+                whole_statistics(b)
+            if r == 3:
+                centre_z(b)
+            if r == 4 or r == 5:
+                for it in range(2 * (r - 4), 2 * (r - 4) + 2):
+                    write_out(b, it)
+            if r == 5 and b == B - 1:
+                write_p_sum()
+
+        x_raw[0] = load_unit(x_view(0))
+        wj_raw = load_unit(permuted_xj_y.rearrange("(c p t) j -> p c t j", c=PASSES, t=PACK))
+        for u in range(1, 1 + LOAD_AHEAD):
+            x_raw[u] = load_unit(x_view(u))
+        x_words[0] = prepare_unit_by_passes(x_raw[0], x_pool, "x")
+        wj_words, wj_scales = prepare_unit_by_passes(wj_raw, const, "wj")
+        wi_raw = load_unit(permuted_xi_y.rearrange("(g t p) i -> p g t i", g=PASSES, t=PACK))
         for step in range(PIECES, AHEAD):
             prepare_x(step)
-        wi_words, wi_scales = quantise_weight(
-            permuted_xi_y.rearrange("(g t p) i -> p g t i", g=PASSES, t=PACK), "wi", PIECE_COLS
-        )
-        gain = const.tile([P, J_TILES, J], BF16)
-        nc.sync.dma_start(out=gain[:], in_=gamma_p.rearrange("(a p) j -> p a j", p=P))
-        bias = const.tile([P, J_TILES, J], BF16)
-        nc.sync.dma_start(out=bias[:], in_=beta_p.rearrange("(a p) j -> p a j", p=P))
-        gain_rows = const.tile([B, J], BF16)
-        nc.sync.dma_start(out=gain_rows[:], in_=gamma_p_sum.partition_broadcast(B))
-        bias_rows = const.tile([B, J], BF16)
-        nc.sync.dma_start(out=bias_rows[:], in_=beta_p_sum.partition_broadcast(B))
 
-        for b in range(B):
+        gain = const.tile([P, J_TILES, J], BF16)
+        bias = const.tile([P, J_TILES, J], BF16)
+        gain_rows = const.tile([B, J], BF16)
+        bias_rows = const.tile([B, J], BF16)
+        bias_plus_one = const.tile([B, J], F32)
+
+        for b in range(B + 1):
             for r in range(ROUNDS):
-                step = b * ROUNDS + r + AHEAD
-                if step <= B * ROUNDS:
-                    prepare_x(step)
-                first_contraction_round(b, r)
-                if b > 0 and r == 1:
-                    second_contraction(b - 1)
-            add_column_sum(b)
-        write_p_sum()
-        second_contraction(B - 1)
+                half = (b * ROUNDS + r) // UNIT_ROUNDS - 1
+                if r % UNIT_ROUNDS == 0 and 0 <= half < UNITS:
+                    quantise_y(*divmod(half, PASSES))
+                if b < B:
+                    step = b * ROUNDS + r + AHEAD
+                    if step <= UNITS * PIECES + 1:
+                        prepare_x(step)
+                    first_contraction_round(b, r)
+                if b == B - 1 and r < B - 1:
+                    add_column_sum(r)
+                if b == 0 and r == WI_ROUND:
+                    wi_grouped = new_grouped()
+                    vector_regroups_rest(wi_raw, wi_grouped, EARLY_PIECE_COLS)
+                    for i in range(PIECES):
+                        scalar_regroups_piece(wi_raw, wi_grouped, i, EARLY_PIECE_COLS)
+                    wi_words, wi_scales = quantise_unit(wi_grouped, const, "wi")
+                    nc.sync.dma_start(out=gain[:], in_=gamma_p.rearrange("(a p) j -> p a j", p=P))
+                    nc.sync.dma_start(out=bias[:], in_=beta_p.rearrange("(a p) j -> p a j", p=P))
+                    nc.sync.dma_start(out=gain_rows[:], in_=gamma_p_sum.partition_broadcast(B))
+                    nc.sync.dma_start(out=bias_rows[:], in_=beta_p_sum.partition_broadcast(B))
+                if b > 0:
+                    finish_item(b - 1, r)

@@ -31,10 +31,11 @@ ROUNDS = PASSES * UNIT_ROUNDS
 PIECES = 2 * PASSES
 FIRST_PIECE_COLS = 128
 EARLY_PIECE_COLS = 80
-PIECE_COLS = 256
+PIECE_COLS = 240
 EARLY_UNITS = 2 * PASSES
 AHEAD = UNIT_ROUNDS + 3
 LOAD_AHEAD = 2
+X_UNITS_ALIVE = 4 * PASSES
 WI_ROUND = 3
 
 FLOPS = B * (2 * M * N * J + 2 * N * J * J)
@@ -48,7 +49,7 @@ def tile_selfprojection_pb_kernel(
         const = stack.enter_context(tc.tile_pool(name="const", bufs=1))
         raw_pool = stack.enter_context(tc.tile_pool(name="raw", bufs=4))
         grouped_pool = stack.enter_context(tc.tile_pool(name="grouped", bufs=3))
-        x_pool = stack.enter_context(tc.tile_pool(name="x_quantised", bufs=4))
+        x_pool = stack.enter_context(tc.tile_pool(name="x_quantised", bufs=X_UNITS_ALIVE))
         y_pool = stack.enter_context(tc.tile_pool(name="y_quantised", bufs=2))
         result = stack.enter_context(tc.tile_pool(name="result", bufs=2))
         stats = stack.enter_context(tc.tile_pool(name="stats", bufs=2))
@@ -136,8 +137,7 @@ def tile_selfprojection_pb_kernel(
                 x_raw[u + LOAD_AHEAD] = load_unit(x_view(u + LOAD_AHEAD))
             if i == 0 and u < UNITS:
                 x_grouped[u] = new_grouped()
-                if u < EARLY_UNITS:
-                    vector_regroups_rest(x_raw[u], x_grouped[u], width)
+                vector_regroups_rest(x_raw[u], x_grouped[u], width)
             if i == 1 and u - 1 not in x_words:
                 x_words[u - 1] = quantise_unit(x_grouped[u - 1], x_pool, "x")
             if u < UNITS:
@@ -158,22 +158,6 @@ def tile_selfprojection_pb_kernel(
                 )
                 y_words[b] = y_pool.tile([P, PASSES, J], U32, name="y_words", align_bytes=64)
                 y_scales[b] = y_pool.tile([P, PASSES, J], U8, name="y_scales", align_bytes=64)
-                column_sum[b] = psum.tile([P, J], F32, name="column_sum")
-
-            rows = slice(jt * P, (jt + 1) * P)
-            for c in range(PASSES):
-                nc.tensor.matmul_mx(
-                    out=column_sum[b][:],
-                    lhsT=words[:, c, rows].bitcast(FP8X4),
-                    lhsT_scale=scales[:, c, rows],
-                    rhs=wj_words[:, c, :].bitcast(FP8X4),
-                    rhs_scale=wj_scales[:, c, :],
-                    start=(r == 0 and c == 0),
-                    stop=(r == ROUNDS - 1 and c == PASSES - 1),
-                )
-            if r == ROUNDS - 1:
-                partial[b] = partials.tile([P, J], F32, name="partial")
-                nc.scalar.copy(out=partial[b][:], in_=column_sum[b][:])
 
             y_bank = psum.tile([P, PACK, P], F32, name="y_bank", tag="work", bufs=3)
             cols = slice(jt * P, (jt + 1) * P)
@@ -192,6 +176,26 @@ def tile_selfprojection_pb_kernel(
             nc.scalar.copy(
                 out=y_grouped[b][:, g, cols, :], in_=y_bank[:].rearrange("p t j -> p j t")
             )
+
+        def column_sum_round(b, r):
+            g, tile_of_unit = divmod(r, UNIT_ROUNDS)
+            words, scales = x_words[b * PASSES + g]
+            if r == 0:
+                column_sum[b] = psum.tile([P, J], F32, name="column_sum")
+            rows = slice(tile_of_unit * P, (tile_of_unit + 1) * P)
+            for c in range(PASSES):
+                nc.tensor.matmul_mx(
+                    out=column_sum[b][:],
+                    lhsT=words[:, c, rows].bitcast(FP8X4),
+                    lhsT_scale=scales[:, c, rows],
+                    rhs=wj_words[:, c, :].bitcast(FP8X4),
+                    rhs_scale=wj_scales[:, c, :],
+                    start=(r == 0 and c == 0),
+                    stop=(r == ROUNDS - 1 and c == PASSES - 1),
+                )
+            if r == ROUNDS - 1:
+                partial[b] = partials.tile([P, J], F32, name="partial")
+                nc.scalar.copy(out=partial[b][:], in_=column_sum[b][:])
 
         def quantise_y(b, g):
             nc.vector.quantize_mx(
@@ -317,12 +321,8 @@ def tile_selfprojection_pb_kernel(
         def finish_item(b, r):
             if r == 0 and b == 0:
                 nc.vector.tensor_scalar_add(out=bias_plus_one[:], in0=bias_rows[:], scalar1=1.0)
-            if r == 0 and b == B - 1:
-                add_column_sum(b)
             if r == 1:
                 second_contraction(b)
-                if b == B - 1:
-                    centre_c()
             if r == 2:
                 whole_statistics(b)
             if r == 3:
@@ -330,8 +330,6 @@ def tile_selfprojection_pb_kernel(
             if r == 4 or r == 5:
                 for it in range(2 * (r - 4), 2 * (r - 4) + 2):
                     write_out(b, it)
-            if r == 5 and b == B - 1:
-                write_p_sum()
 
         x_raw[0] = load_unit(x_view(0))
         wj_raw = load_unit(permuted_xj_y.rearrange("(c p t) j -> p c t j", c=PASSES, t=PACK))
@@ -359,8 +357,6 @@ def tile_selfprojection_pb_kernel(
                     if step <= UNITS * PIECES + 1:
                         prepare_x(step)
                     first_contraction_round(b, r)
-                if b == B - 1 and r < B - 1:
-                    add_column_sum(r)
                 if b == 0 and r == WI_ROUND:
                     wi_grouped = new_grouped()
                     vector_regroups_rest(wi_raw, wi_grouped, EARLY_PIECE_COLS)
@@ -372,4 +368,10 @@ def tile_selfprojection_pb_kernel(
                     nc.sync.dma_start(out=gain_rows[:], in_=gamma_p_sum.partition_broadcast(B))
                     nc.sync.dma_start(out=bias_rows[:], in_=beta_p_sum.partition_broadcast(B))
                 if b > 0:
+                    column_sum_round(b - 1, r)
                     finish_item(b - 1, r)
+
+        for b in range(B):
+            add_column_sum(b)
+        centre_c()
+        write_p_sum()

@@ -31,7 +31,7 @@ ROUNDS = PASSES * UNIT_ROUNDS
 PIECES = 2 * PASSES
 FIRST_PIECE_COLS = 128
 EARLY_PIECE_COLS = 80
-PIECE_COLS = 240
+PIECE_COLS = 208
 EARLY_UNITS = 2 * PASSES
 AHEAD = UNIT_ROUNDS + 3
 LOAD_AHEAD = 2

@@ -1,7 +1,7 @@
+import math
 from contextlib import ExitStack
 
 import concourse.mybir as mybir
-from concourse.masks import make_identity
 
 F32 = mybir.dt.float32
 BF16 = mybir.dt.bfloat16
@@ -10,7 +10,6 @@ U8 = mybir.dt.uint8
 FP8X4 = mybir.dt.float8_e4m3fn_x4
 ALU = mybir.AluOpType
 ACT = mybir.ActivationFunctionType
-AXIS = mybir.AxisListType
 
 B = 6
 M = 1024
@@ -61,8 +60,8 @@ def tile_selfprojection_pb_kernel(
         warm = const.tile([P, 1], F32)
         nc.scalar.activation(out=warm[:], in_=one[:], func=ACT.Sqrt)
 
-        identity = const.tile([P, P], F32)
-        make_identity(nc, identity[:])
+        one_over_p = const.tile([P, P], F32)
+        nc.vector.memset(one_over_p[:], 1.0 / P)
         pick = const.tile([P, 2 * P], F32)
         nc.vector.memset(pick[:], 0.0)
         nc.vector.memset(pick[:, P : P + 1], 1.0)
@@ -254,7 +253,7 @@ def tile_selfprojection_pb_kernel(
         z_banks = {}
         z_mean_var = {}
         z_whole = {}
-        z_std = {}
+        z_padded = {}
         z_inverse = {}
         centred = {}
         normal = {}
@@ -279,27 +278,29 @@ def tile_selfprojection_pb_kernel(
             nc.vector.bn_aggr(out=z_mean_var[b][:], in_=six[:].rearrange("p a s -> p (a s)"))
 
         def whole_statistics(b):
-            spread = psum.tile([P, 2, P], F32, name="spread", tag="work", bufs=3)
-            for s in range(2):
-                nc.tensor.matmul(
-                    out=spread[:, s, :],
-                    lhsT=z_mean_var[b][:, s : s + 1].to_broadcast([P, P]),
-                    rhs=identity[:],
-                    start=True,
-                    stop=True,
-                )
-            means_six = stats.tile([P, 6], F32, name="means_six")
-            nc.vector.bn_stats(out=means_six[:], in_=spread[:, 0, :])
-            z_whole[b] = stats.tile([P, 2], F32, name="whole")
-            nc.vector.bn_aggr(out=z_whole[b][:], in_=means_six[:])
-            var_sum = stats.tile([P, 1], F32, name="var_sum")
-            nc.vector.reduce_sum(out=var_sum[:], in_=spread[:, 1, :], axis=AXIS.X)
-            population_var = stats.tile([P, 1], F32, name="population_var")
-            nc.vector.tensor_scalar(
-                out=population_var[:], in0=var_sum[:], scalar1=1.0 / P,
-                scalar2=z_whole[b][:, 1:2], op0=ALU.mult, op1=ALU.add,
+            averages = psum.tile([P, 3], F32, name="averages", tag="work", bufs=3)
+            nc.tensor.matmul(
+                out=averages[:, 0:2], lhsT=one_over_p[:], rhs=z_mean_var[b][:], start=True, stop=True
             )
-            z_std[b] = std_of(population_var[:], J * J, P)
+            z_whole[b] = stats.tile([P, 2], F32, name="whole")
+            nc.scalar.copy(out=z_whole[b][:], in_=averages[:, 0:2])
+            distance = stats.tile([P, 1], F32, name="distance")
+            nc.scalar.activation(
+                out=distance[:], in_=z_mean_var[b][:, 0:1], func=ACT.Square,
+                scale=-1.0, bias=z_whole[b][:, 0:1],
+            )
+            nc.tensor.matmul(
+                out=averages[:, 2:3], lhsT=one_over_p[:], rhs=distance[:], start=True, stop=True
+            )
+            std = stats.tile([P, 1], F32, name="z_std")
+            nc.scalar.activation(
+                out=std[:], in_=averages[:, 2:3], func=ACT.Sqrt, bias=z_whole[b][:, 1:2]
+            )
+            z_padded[b] = stats.tile([P, 1], F32, name="z_padded")
+            nc.scalar.activation(
+                out=z_padded[b][:], in_=std[:], func=ACT.Identity,
+                scale=math.sqrt(J * J / (J * J - 1.0)), bias=EPS,
+            )
 
         def centre_z(b):
             centred[b] = result.tile([P, J_TILES, J], F32, name="centred")
@@ -308,7 +309,8 @@ def tile_selfprojection_pb_kernel(
                     out=centred[b][:, it, :], in0=z_banks[b, it][:], scalar=z_whole[b][:, 0:1],
                     in1=gain[:, it, :], op0=ALU.subtract, op1=ALU.mult,
                 )
-            z_inverse[b] = inverse_of(z_std[b], P)
+            z_inverse[b] = stats.tile([P, 1], F32, name="z_inverse")
+            nc.vector.reciprocal(out=z_inverse[b][:], in_=z_padded[b][:])
             normal[b] = result.tile([P, J_TILES, J], F32, name="normal")
 
         def write_out(b, it):

@@ -2,6 +2,7 @@ import math
 from contextlib import ExitStack
 
 import concourse.mybir as mybir
+from concourse.masks import make_identity
 
 F32 = mybir.dt.float32
 BF16 = mybir.dt.bfloat16
@@ -10,6 +11,7 @@ U8 = mybir.dt.uint8
 FP8X4 = mybir.dt.float8_e4m3fn_x4
 ALU = mybir.AluOpType
 ACT = mybir.ActivationFunctionType
+AXIS = mybir.AxisListType
 
 B = 6
 M = 1024
@@ -30,12 +32,19 @@ ROUNDS = PASSES * UNIT_ROUNDS
 PIECES = 2 * PASSES
 FIRST_PIECE_COLS = 128
 EARLY_PIECE_COLS = 80
-PIECE_COLS = 208
+PIECE_COLS = 176
 EARLY_UNITS = 2 * PASSES
 AHEAD = UNIT_ROUNDS + 3
 LOAD_AHEAD = 2
-X_UNITS_ALIVE = 4 * PASSES
+X_UNITS_ALIVE = 3 * PASSES
 WI_ROUND = 3
+PAIRS = J_TILES // 2
+Y_BANKS = 2
+TURN_BANKS = 2
+TURN_LAG = 2
+VECTOR_TURNS = ()
+Z_ROUND = 2
+P_SUM_ROUND = 2
 
 FLOPS = B * (2 * M * N * J + 2 * N * J * J)
 
@@ -52,7 +61,6 @@ def tile_selfprojection_pb_kernel(
         y_pool = stack.enter_context(tc.tile_pool(name="y_quantised", bufs=2))
         result = stack.enter_context(tc.tile_pool(name="result", bufs=2))
         stats = stack.enter_context(tc.tile_pool(name="stats", bufs=2))
-        partials = stack.enter_context(tc.tile_pool(name="partials", bufs=B))
         psum = stack.enter_context(tc.psum_pool(name="psum", bufs=1))
 
         one = const.tile([P, 1], F32)
@@ -62,9 +70,10 @@ def tile_selfprojection_pb_kernel(
 
         one_over_p = const.tile([P, P], F32)
         nc.vector.memset(one_over_p[:], 1.0 / P)
-        pick = const.tile([P, 2 * P], F32)
-        nc.vector.memset(pick[:], 0.0)
-        nc.vector.memset(pick[:, P : P + 1], 1.0)
+        identity = const.tile([P, P], F32)
+        make_identity(nc, identity[:])
+        one_over_j = const.tile([P, P], F32)
+        nc.vector.memset(one_over_j[:], 1.0 / J)
 
         def load_unit(view):
             raw = raw_pool.tile([P, PASSES, PACK, J], BF16, name="raw")
@@ -125,6 +134,7 @@ def tile_selfprojection_pb_kernel(
                 )
             return words, scales
 
+        c_parts = const.tile([P, B, J_TILES, PASSES], F32)
         x_raw = {}
         x_grouped = {}
         x_words = {}
@@ -142,59 +152,56 @@ def tile_selfprojection_pb_kernel(
             if u < UNITS:
                 scalar_regroups_piece(x_raw[u], x_grouped[u], i, width)
 
+        y_rows = {}
         y_grouped = {}
         y_words = {}
         y_scales = {}
-        column_sum = {}
-        partial = {}
 
         def first_contraction_round(b, r):
             g, jt = divmod(r, UNIT_ROUNDS)
             words, scales = x_words[b * PASSES + g]
             if r == 0:
+                y_rows[b] = y_pool.tile([P, J_TILES, N], BF16, name="y_rows", align_bytes=64)
                 y_grouped[b] = y_pool.tile(
                     [P, PASSES, J, PACK], BF16, name="y_grouped", align_bytes=64
                 )
                 y_words[b] = y_pool.tile([P, PASSES, J], U32, name="y_words", align_bytes=64)
                 y_scales[b] = y_pool.tile([P, PASSES, J], U8, name="y_scales", align_bytes=64)
-
-            y_bank = psum.tile([P, PACK, P], F32, name="y_bank", tag="work", bufs=3)
+            y_bank = psum.tile([P, J], F32, name="y_bank", bufs=Y_BANKS)
             cols = slice(jt * P, (jt + 1) * P)
-            for t in range(PACK):
-                rows = slice(t * P, (t + 1) * P)
-                for c in range(PASSES):
-                    nc.tensor.matmul_mx(
-                        out=y_bank[:, t, :],
-                        lhsT=words[:, c, rows].bitcast(FP8X4),
-                        lhsT_scale=scales[:, c, rows],
-                        rhs=wj_words[:, c, cols].bitcast(FP8X4),
-                        rhs_scale=wj_scales[:, c, cols],
-                        start=(c == 0),
-                        stop=(c == PASSES - 1),
-                    )
-            nc.scalar.copy(
-                out=y_grouped[b][:, g, cols, :], in_=y_bank[:].rearrange("p t j -> p j t")
-            )
-
-        def column_sum_round(b, r):
-            g, tile_of_unit = divmod(r, UNIT_ROUNDS)
-            words, scales = x_words[b * PASSES + g]
-            if r == 0:
-                column_sum[b] = psum.tile([P, J], F32, name="column_sum")
-            rows = slice(tile_of_unit * P, (tile_of_unit + 1) * P)
             for c in range(PASSES):
                 nc.tensor.matmul_mx(
-                    out=column_sum[b][:],
-                    lhsT=words[:, c, rows].bitcast(FP8X4),
-                    lhsT_scale=scales[:, c, rows],
-                    rhs=wj_words[:, c, :].bitcast(FP8X4),
-                    rhs_scale=wj_scales[:, c, :],
-                    start=(r == 0 and c == 0),
-                    stop=(r == ROUNDS - 1 and c == PASSES - 1),
+                    out=y_bank[:],
+                    lhsT=wj_words[:, c, cols].bitcast(FP8X4),
+                    lhsT_scale=wj_scales[:, c, cols],
+                    rhs=words[:, c, :].bitcast(FP8X4),
+                    rhs_scale=scales[:, c, :],
+                    start=(c == 0),
+                    stop=(c == PASSES - 1),
                 )
-            if r == ROUNDS - 1:
-                partial[b] = partials.tile([P, J], F32, name="partial")
-                nc.scalar.copy(out=partial[b][:], in_=column_sum[b][:])
+            nc.scalar.activation(
+                out=y_rows[b][:, jt, g * J : (g + 1) * J], in_=y_bank[:], func=ACT.Identity,
+                accum_out=c_parts[:, b, jt, g : g + 1],
+            )
+
+        def turn_round(b, k):
+            g, pair = divmod(k, PAIRS)
+            turned = psum.tile([P, 2, 2, P], F32, name="turned", bufs=TURN_BANKS)
+            for i in range(2):
+                jt = 2 * pair + i
+                row_words = y_rows[b][:, jt, :].bitcast(F32)
+                for u in range(2):
+                    start = g * (J // 2) + u * P
+                    nc.tensor.transpose(
+                        turned[:, i, u, :], row_words[:, start : start + P], identity[:]
+                    )
+            cols = slice(2 * pair * P, 2 * (pair + 1) * P)
+            out = y_grouped[b][:, g, cols, :].rearrange("p j t -> p (j t)").bitcast(F32)
+            copy = nc.vector.tensor_copy if k in VECTOR_TURNS else nc.scalar.copy
+            copy(
+                out=out.rearrange("p (i j u) -> p i j u", i=2, u=2),
+                in_=turned[:].rearrange("p i u j -> p i j u"),
+            )
 
         def quantise_y(b, g):
             nc.vector.quantize_mx(
@@ -203,52 +210,47 @@ def tile_selfprojection_pb_kernel(
                 in_=y_grouped[b][:, g].rearrange("p j t -> p (j t)"),
             )
 
-        c_rows = {}
+        c_columns = const.tile([P, P // J_TILES, J_TILES], F32)
+        nc.vector.memset(c_columns[:], 0.0)
 
-        def add_column_sum(b):
-            if b == 0:
-                c_rows[0] = psum.tile([P, J], F32, name="c_bank", tag="work", bufs=3)
+        def mean_of_items(columns, name):
+            sums = psum.tile([P, B * J_TILES], F32, name="sums", tag="turned", bufs=TURN_BANKS)
             nc.tensor.matmul(
-                out=c_rows[0][:], lhsT=pick[:, P - b : 2 * P - b], rhs=partial[b][:],
-                start=(b == 0), stop=(b == B - 1),
+                out=sums[:], lhsT=one_over_j[:], rhs=columns.rearrange("p b t -> p (b t)"),
+                start=True, stop=True,
             )
-
-        def std_of(population_var, count, rows):
-            std = stats.tile([P, 1], F32, name="std")
-            nc.scalar.activation(
-                out=std[:rows], in_=population_var, func=ACT.Sqrt, scale=count / (count - 1.0)
+            mean = const.tile([P, B], F32, name=name)
+            nc.vector.reduce_sum(
+                out=mean[:], in_=sums[:].rearrange("p (b t) -> p b t", t=J_TILES), axis=AXIS.X
             )
-            return std
+            return mean
 
-        def inverse_of(std, rows):
-            padded = stats.tile([P, 1], F32, name="padded")
-            nc.vector.tensor_scalar_add(out=padded[:rows], in0=std[:rows], scalar1=EPS)
-            inverse = stats.tile([P, 1], F32, name="inverse")
-            nc.vector.reciprocal(out=inverse[:rows], in_=padded[:rows])
-            return inverse
-
-        c_centred = const.tile([B, J], F32)
-        c_std = {}
-
-        def centre_c():
-            six = stats.tile([P, 6], F32, name="c_six")
-            nc.vector.bn_stats(out=six[:B], in_=c_rows[0][:B, :])
-            mean_var = stats.tile([P, 2], F32, name="c_mean_var")
-            nc.vector.bn_aggr(out=mean_var[:B], in_=six[:B])
-            c_std[0] = std_of(mean_var[:B, 1:2], J, B)
-            nc.vector.scalar_tensor_tensor(
-                out=c_centred[:], in0=c_rows[0][:B, :], scalar=mean_var[:B, 0:1], in1=gain_rows[:],
-                op0=ALU.subtract, op1=ALU.mult,
-            )
+        def spread_over_tiles(values):
+            return values[:].unsqueeze(2).to_broadcast([P, B, J_TILES])
 
         def write_p_sum():
-            inverse = inverse_of(c_std[0], B)
-            p_sum = const.tile([B, J], F32)
-            nc.vector.scalar_tensor_tensor(
-                out=p_sum[:], in0=c_centred[:], scalar=inverse[:B, 0:1], in1=bias_plus_one[:],
-                op0=ALU.mult, op1=ALU.add,
+            used = c_columns[:, :B, :]
+            nc.vector.reduce_sum(out=used, in_=c_parts[:], axis=AXIS.X)
+            mean = mean_of_items(used, "c_mean")
+            nc.vector.tensor_sub(out=used, in0=used, in1=spread_over_tiles(mean))
+            squares = const.tile([P, B, J_TILES], F32)
+            nc.vector.tensor_mul(out=squares[:], in0=used, in1=used)
+            variance = mean_of_items(squares[:], "c_variance")
+            std = const.tile([P, B], F32, name="c_std")
+            nc.scalar.activation(
+                out=std[:], in_=variance[:], func=ACT.Sqrt, scale=J / (J - 1.0)
             )
-            nc.sync.dma_start(out=out_1, in_=p_sum[:])
+            padded = const.tile([P, B], F32, name="c_padded")
+            nc.vector.tensor_scalar_add(out=padded[:], in0=std[:], scalar1=EPS)
+            inverse = const.tile([P, B], F32, name="c_inverse")
+            nc.vector.reciprocal(out=inverse[:], in_=padded[:])
+            nc.vector.tensor_mul(out=used, in0=used, in1=spread_over_tiles(inverse))
+            rows = psum.tile([P, P], F32, name="rows", tag="turned", bufs=TURN_BANKS)
+            nc.tensor.transpose(rows[:], c_columns[:].rearrange("p b t -> p (b t)"), identity[:])
+            p_sum = const.tile([B * J_TILES, P], F32)
+            nc.vector.tensor_mul(out=p_sum[:], in0=rows[: B * J_TILES, :], in1=gain_rows[:])
+            nc.vector.tensor_add(out=p_sum[:], in0=p_sum[:], in1=bias_plus_one[:])
+            nc.sync.dma_start(out=out_1.rearrange("b (t j) -> (b t) j", j=P), in_=p_sum[:])
 
         z_banks = {}
         z_mean_var = {}
@@ -278,7 +280,7 @@ def tile_selfprojection_pb_kernel(
             nc.vector.bn_aggr(out=z_mean_var[b][:], in_=six[:].rearrange("p a s -> p (a s)"))
 
         def whole_statistics(b):
-            averages = psum.tile([P, 3], F32, name="averages", tag="work", bufs=3)
+            averages = psum.tile([P, 3], F32, name="averages", tag="turned", bufs=TURN_BANKS)
             nc.tensor.matmul(
                 out=averages[:, 0:2], lhsT=one_over_p[:], rhs=z_mean_var[b][:], start=True, stop=True
             )
@@ -323,15 +325,17 @@ def tile_selfprojection_pb_kernel(
         def finish_item(b, r):
             if r == 0 and b == 0:
                 nc.vector.tensor_scalar_add(out=bias_plus_one[:], in0=bias_rows[:], scalar1=1.0)
-            if r == 1:
+            if r == 0 + Z_ROUND:
                 second_contraction(b)
-            if r == 2:
+            if r == 1 + Z_ROUND:
                 whole_statistics(b)
-            if r == 3:
+            if r == 2 + Z_ROUND:
                 centre_z(b)
-            if r == 4 or r == 5:
-                for it in range(2 * (r - 4), 2 * (r - 4) + 2):
+            if r == 3 + Z_ROUND or r == 4 + Z_ROUND:
+                for it in range(2 * (r - 3 - Z_ROUND), 2 * (r - 3 - Z_ROUND) + 2):
                     write_out(b, it)
+            if r == P_SUM_ROUND and b == B - 1:
+                write_p_sum()
 
         x_raw[0] = load_unit(x_view(0))
         wj_raw = load_unit(permuted_xj_y.rearrange("(c p t) j -> p c t j", c=PASSES, t=PACK))
@@ -339,21 +343,29 @@ def tile_selfprojection_pb_kernel(
             x_raw[u] = load_unit(x_view(u))
         x_words[0] = prepare_unit_by_passes(x_raw[0], x_pool, "x")
         wj_words, wj_scales = prepare_unit_by_passes(wj_raw, const, "wj")
-        wi_raw = load_unit(permuted_xi_y.rearrange("(g t p) i -> p g t i", g=PASSES, t=PACK))
+        wi_raw = raw_pool.tile([P, PASSES, PACK, J], BF16, name="raw")
+        wi_view = permuted_xi_y.rearrange("(g u p e) i -> p g u (e i)", g=PASSES, u=2, e=2)
+        for g in range(PASSES):
+            nc.sync.dma_start(
+                out=wi_raw[:, g].rearrange("p (u e) i -> p u (e i)", e=2), in_=wi_view[:, g]
+            )
         for step in range(PIECES, AHEAD):
             prepare_x(step)
 
         gain = const.tile([P, J_TILES, J], BF16)
         bias = const.tile([P, J_TILES, J], BF16)
-        gain_rows = const.tile([B, J], BF16)
-        bias_rows = const.tile([B, J], BF16)
-        bias_plus_one = const.tile([B, J], F32)
+        gain_rows = const.tile([B * J_TILES, P], BF16)
+        bias_rows = const.tile([B * J_TILES, P], BF16)
+        bias_plus_one = const.tile([B * J_TILES, P], F32)
 
         for b in range(B + 1):
             for r in range(ROUNDS):
-                half = (b * ROUNDS + r) // UNIT_ROUNDS - 1
-                if r % UNIT_ROUNDS == 0 and 0 <= half < UNITS:
-                    quantise_y(*divmod(half, PASSES))
+                turn = b * ROUNDS + r - 1 - TURN_LAG
+                if turn % 2 == 0 and 0 <= turn // 2 < UNITS * PAIRS:
+                    item, k = divmod(turn // 2, PASSES * PAIRS)
+                    turn_round(item, k)
+                    if k % PAIRS == PAIRS - 1:
+                        quantise_y(item, k // PAIRS)
                 if b < B:
                     step = b * ROUNDS + r + AHEAD
                     if step <= UNITS * PIECES + 1:
@@ -367,13 +379,13 @@ def tile_selfprojection_pb_kernel(
                     wi_words, wi_scales = quantise_unit(wi_grouped, const, "wi")
                     nc.sync.dma_start(out=gain[:], in_=gamma_p.rearrange("(a p) j -> p a j", p=P))
                     nc.sync.dma_start(out=bias[:], in_=beta_p.rearrange("(a p) j -> p a j", p=P))
-                    nc.sync.dma_start(out=gain_rows[:], in_=gamma_p_sum.partition_broadcast(B))
-                    nc.sync.dma_start(out=bias_rows[:], in_=beta_p_sum.partition_broadcast(B))
+                    for item in range(B):
+                        rows = slice(item * J_TILES, (item + 1) * J_TILES)
+                        nc.sync.dma_start(
+                            out=gain_rows[rows, :], in_=gamma_p_sum.rearrange("(t j) -> t j", j=P)
+                        )
+                        nc.sync.dma_start(
+                            out=bias_rows[rows, :], in_=beta_p_sum.rearrange("(t j) -> t j", j=P)
+                        )
                 if b > 0:
-                    column_sum_round(b - 1, r)
                     finish_item(b - 1, r)
-
-        for b in range(B):
-            add_column_sum(b)
-        centre_c()
-        write_p_sum()

@@ -31,8 +31,8 @@ UNIT_ROUNDS = J_TILES
 ROUNDS = PASSES * UNIT_ROUNDS
 PIECES = 2 * PASSES
 FIRST_PIECE_COLS = 128
-EARLY_PIECE_COLS = 80
-PIECE_COLS = 176
+EARLY_PIECE_COLS = 64
+PIECE_COLS = 160
 EARLY_UNITS = 2 * PASSES
 AHEAD = UNIT_ROUNDS + 3
 LOAD_AHEAD = 2

@@ -32,7 +32,7 @@ ROUNDS = PASSES * UNIT_ROUNDS
 PIECES = 2 * PASSES
 FIRST_PIECE_COLS = 128
 EARLY_PIECE_COLS = 64
-PIECE_COLS = 160
+PIECE_COLS = 152
 EARLY_UNITS = 2 * PASSES
 AHEAD = UNIT_ROUNDS + 3
 LOAD_AHEAD = 2
@@ -43,7 +43,7 @@ Y_BANKS = 2
 TURN_BANKS = 2
 TURN_LAG = 2
 VECTOR_TURNS = ()
-Z_ROUND = 2
+Z_ROUND = 3
 P_SUM_ROUND = 2
 
 FLOPS = B * (2 * M * N * J + 2 * N * J * J)
@@ -315,12 +315,16 @@ def tile_selfprojection_pb_kernel(
             nc.vector.reciprocal(out=z_inverse[b][:], in_=z_padded[b][:])
             normal[b] = result.tile([P, J_TILES, J], F32, name="normal")
 
-        def write_out(b, it):
+        def write_out(b, first, count):
+            tiles = slice(first, first + count)
             nc.vector.scalar_tensor_tensor(
-                out=normal[b][:, it, :], in0=centred[b][:, it, :], scalar=z_inverse[b][:, 0:1],
-                in1=bias[:, it, :], op0=ALU.mult, op1=ALU.add,
+                out=normal[b][:, tiles, :], in0=centred[b][:, tiles, :],
+                scalar=z_inverse[b][:, 0:1], in1=bias[:, tiles, :], op0=ALU.mult, op1=ALU.add,
             )
-            nc.sync.dma_start(out=out_0[b, it * P : (it + 1) * P, :], in_=normal[b][:, it, :])
+            nc.sync.dma_start(
+                out=out_0[b, first * P : (first + count) * P, :].rearrange("(a p) j -> p a j", p=P),
+                in_=normal[b][:, tiles, :],
+            )
 
         def finish_item(b, r):
             if r == 0 and b == 0:
@@ -332,8 +336,12 @@ def tile_selfprojection_pb_kernel(
             if r == 2 + Z_ROUND:
                 centre_z(b)
             if r == 3 + Z_ROUND or r == 4 + Z_ROUND:
-                for it in range(2 * (r - 3 - Z_ROUND), 2 * (r - 3 - Z_ROUND) + 2):
-                    write_out(b, it)
+                pair = 2 * (r - 3 - Z_ROUND)
+                if b < B - 1:
+                    write_out(b, pair, 2)
+                else:
+                    write_out(b, pair, 1)
+                    write_out(b, pair + 1, 1)
             if r == P_SUM_ROUND and b == B - 1:
                 write_p_sum()
 

@@ -32,16 +32,17 @@ ROUNDS = PASSES * UNIT_ROUNDS
 PIECES = 2 * PASSES
 FIRST_PIECE_COLS = 128
 EARLY_PIECE_COLS = 64
-PIECE_COLS = 152
+PIECE_COLS = 144
 EARLY_UNITS = 2 * PASSES
 AHEAD = UNIT_ROUNDS + 3
-LOAD_AHEAD = 2
+LOAD_AHEAD = 3
 X_UNITS_ALIVE = 3 * PASSES
-WI_ROUND = 3
+WI_ROUND = 5
+GAIN_ROUND = 6
 PAIRS = J_TILES // 2
 Y_BANKS = 2
 TURN_BANKS = 2
-TURN_LAG = 2
+TURN_LAG = 1
 VECTOR_TURNS = ()
 Z_ROUND = 3
 P_SUM_ROUND = 2
@@ -55,13 +56,15 @@ def tile_selfprojection_pb_kernel(
     nc = tc.nc
     with ExitStack() as stack:
         const = stack.enter_context(tc.tile_pool(name="const", bufs=1))
-        raw_pool = stack.enter_context(tc.tile_pool(name="raw", bufs=4))
+        raw_pool = stack.enter_context(tc.tile_pool(name="raw", bufs=5))
         grouped_pool = stack.enter_context(tc.tile_pool(name="grouped", bufs=3))
         x_pool = stack.enter_context(tc.tile_pool(name="x_quantised", bufs=X_UNITS_ALIVE))
         y_pool = stack.enter_context(tc.tile_pool(name="y_quantised", bufs=2))
         result = stack.enter_context(tc.tile_pool(name="result", bufs=2))
         stats = stack.enter_context(tc.tile_pool(name="stats", bufs=2))
         psum = stack.enter_context(tc.psum_pool(name="psum", bufs=1))
+
+        stack.enter_context(tc.manual_schedule(engines={mybir.EngineType.SP}))
 
         one = const.tile([P, 1], F32)
         nc.vector.memset(one[:], 1.0)
@@ -366,6 +369,18 @@ def tile_selfprojection_pb_kernel(
         bias_rows = const.tile([B * J_TILES, P], BF16)
         bias_plus_one = const.tile([B * J_TILES, P], F32)
 
+        def load_gains():
+            nc.sync.dma_start(out=gain[:], in_=gamma_p.rearrange("(a p) j -> p a j", p=P))
+            nc.sync.dma_start(out=bias[:], in_=beta_p.rearrange("(a p) j -> p a j", p=P))
+            for item in range(B):
+                rows = slice(item * J_TILES, (item + 1) * J_TILES)
+                nc.sync.dma_start(
+                    out=gain_rows[rows, :], in_=gamma_p_sum.rearrange("(t j) -> t j", j=P)
+                )
+                nc.sync.dma_start(
+                    out=bias_rows[rows, :], in_=beta_p_sum.rearrange("(t j) -> t j", j=P)
+                )
+
         for b in range(B + 1):
             for r in range(ROUNDS):
                 turn = b * ROUNDS + r - 1 - TURN_LAG
@@ -385,15 +400,7 @@ def tile_selfprojection_pb_kernel(
                     for i in range(PIECES):
                         scalar_regroups_piece(wi_raw, wi_grouped, i, EARLY_PIECE_COLS)
                     wi_words, wi_scales = quantise_unit(wi_grouped, const, "wi")
-                    nc.sync.dma_start(out=gain[:], in_=gamma_p.rearrange("(a p) j -> p a j", p=P))
-                    nc.sync.dma_start(out=bias[:], in_=beta_p.rearrange("(a p) j -> p a j", p=P))
-                    for item in range(B):
-                        rows = slice(item * J_TILES, (item + 1) * J_TILES)
-                        nc.sync.dma_start(
-                            out=gain_rows[rows, :], in_=gamma_p_sum.rearrange("(t j) -> t j", j=P)
-                        )
-                        nc.sync.dma_start(
-                            out=bias_rows[rows, :], in_=beta_p_sum.rearrange("(t j) -> t j", j=P)
-                        )
+                if b * ROUNDS + r == GAIN_ROUND:
+                    load_gains()
                 if b > 0:
                     finish_item(b - 1, r)

@@ -30,8 +30,8 @@ UNITS = B * PASSES
 UNIT_ROUNDS = J_TILES
 ROUNDS = PASSES * UNIT_ROUNDS
 PIECES = 2 * PASSES
-FIRST_PIECE_COLS = 128
-EARLY_PIECE_COLS = 64
+FIRST_PIECE_COLS = 112
+EARLY_PIECE_COLS = 48
 PIECE_COLS = 144
 EARLY_UNITS = 2 * PASSES
 AHEAD = UNIT_ROUNDS + 3
@@ -340,11 +340,11 @@ def tile_selfprojection_pb_kernel(
                 centre_z(b)
             if r == 3 + Z_ROUND or r == 4 + Z_ROUND:
                 pair = 2 * (r - 3 - Z_ROUND)
-                if b < B - 1:
-                    write_out(b, pair, 2)
-                else:
+                if b == B - 1:
                     write_out(b, pair, 1)
                     write_out(b, pair + 1, 1)
+                elif pair == 0:
+                    write_out(b, 0, J_TILES)
             if r == P_SUM_ROUND and b == B - 1:
                 write_p_sum()
 

import math
from contextlib import ExitStack

import concourse.mybir as mybir
from concourse.masks import make_identity

F32 = mybir.dt.float32
BF16 = mybir.dt.bfloat16
U32 = mybir.dt.uint32
U8 = mybir.dt.uint8
FP8X4 = mybir.dt.float8_e4m3fn_x4
ALU = mybir.AluOpType
ACT = mybir.ActivationFunctionType
AXIS = mybir.AxisListType

B = 6
M = 1024
N = 1024
J = 512
EPS = 1e-05

P = 128
PACK = 4
K_PASS = P * PACK
PASSES = M // K_PASS
J_TILES = J // P
RUN = 4

UNITS = B * PASSES
UNIT_ROUNDS = J_TILES
ROUNDS = PASSES * UNIT_ROUNDS
PIECES = 2 * PASSES
FIRST_PIECE_COLS = 112
EARLY_PIECE_COLS = 48
PIECE_COLS = 144
EARLY_UNITS = 2 * PASSES
AHEAD = UNIT_ROUNDS + 3
LOAD_AHEAD = 3
X_UNITS_ALIVE = 3 * PASSES
WI_ROUND = 5
GAIN_ROUND = 6
PAIRS = J_TILES // 2
Y_BANKS = 2
TURN_BANKS = 2
TURN_LAG = 1
VECTOR_TURNS = ()
Z_ROUND = 3
P_SUM_ROUND = 2

FLOPS = B * (2 * M * N * J + 2 * N * J * J)


def tile_selfprojection_pb_kernel(
    tc, x, permuted_xj_y, permuted_xi_y, gamma_p_sum, gamma_p, beta_p_sum, beta_p, out_0, out_1
):
    nc = tc.nc
    with ExitStack() as stack:
        const = stack.enter_context(tc.tile_pool(name="const", bufs=1))
        raw_pool = stack.enter_context(tc.tile_pool(name="raw", bufs=5))
        grouped_pool = stack.enter_context(tc.tile_pool(name="grouped", bufs=3))
        x_pool = stack.enter_context(tc.tile_pool(name="x_quantised", bufs=X_UNITS_ALIVE))
        y_pool = stack.enter_context(tc.tile_pool(name="y_quantised", bufs=2))
        result = stack.enter_context(tc.tile_pool(name="result", bufs=2))
        stats = stack.enter_context(tc.tile_pool(name="stats", bufs=2))
        psum = stack.enter_context(tc.psum_pool(name="psum", bufs=1))

        stack.enter_context(tc.manual_schedule(engines={mybir.EngineType.SP}))

        one = const.tile([P, 1], F32)
        nc.vector.memset(one[:], 1.0)
        warm = const.tile([P, 1], F32)
        nc.scalar.activation(out=warm[:], in_=one[:], func=ACT.Sqrt)

        one_over_p = const.tile([P, P], F32)
        nc.vector.memset(one_over_p[:], 1.0 / P)
        identity = const.tile([P, P], F32)
        make_identity(nc, identity[:])
        one_over_j = const.tile([P, P], F32)
        nc.vector.memset(one_over_j[:], 1.0 / J)

        def load_unit(view):
            raw = raw_pool.tile([P, PASSES, PACK, J], BF16, name="raw")
            for c in range(PASSES):
                nc.sync.dma_start(out=raw[:, c], in_=view[:, c])
            return raw

        def x_view(u):
            b, g = divmod(u, PASSES)
            return x[b, :, g * J : (g + 1) * J].rearrange("(c p t) n -> p c t n", c=PASSES, t=PACK)

        def new_grouped():
            return grouped_pool.tile([P, PASSES, J, PACK], BF16, name="grouped", align_bytes=64)

        def vector_regroups_rest(raw, grouped, width):
            nc.vector.tensor_copy(
                out=grouped[:, :, 2 * width :, :].rearrange("p c (k i) t -> p c k t i", i=RUN),
                in_=raw[:, :, :, 2 * width :].rearrange("p c t (k i) -> p c k t i", i=RUN),
            )

        def scalar_regroups_piece(raw, grouped, i, width):
            c, half = divmod(i, 2)
            cols = slice(half * width, (half + 1) * width)
            nc.scalar.copy(
                out=grouped[:, c, cols, :].rearrange("p (k i) t -> p k t i", i=RUN),
                in_=raw[:, c, :, cols].rearrange("p t (k i) -> p k t i", i=RUN),
            )

        def quantise_unit(grouped, pool, name):
            words = pool.tile([P, PASSES, J], U32, name=name + "_words", align_bytes=64)
            scales = pool.tile([P, PASSES, J], U8, name=name + "_scales", align_bytes=64)
            nc.vector.quantize_mx(
                out=words[:].rearrange("p c w -> p (c w)").bitcast(FP8X4),
                scales=scales[:].rearrange("p c w -> p (c w)"),
                in_=grouped[:].rearrange("p c w t -> p (c w t)"),
            )
            return words, scales

        def prepare_unit_by_passes(raw, pool, name):
            grouped = new_grouped()
            words = pool.tile([P, PASSES, J], U32, name=name + "_words", align_bytes=64)
            scales = pool.tile([P, PASSES, J], U8, name=name + "_scales", align_bytes=64)
            for c in range(PASSES):
                nc.vector.tensor_copy(
                    out=grouped[:, c, 2 * FIRST_PIECE_COLS :, :].rearrange(
                        "p (k i) t -> p k t i", i=RUN
                    ),
                    in_=raw[:, c, :, 2 * FIRST_PIECE_COLS :].rearrange(
                        "p t (k i) -> p k t i", i=RUN
                    ),
                )
                for i in range(2 * c, 2 * c + 2):
                    scalar_regroups_piece(raw, grouped, i, FIRST_PIECE_COLS)
                nc.vector.quantize_mx(
                    out=words[:, c, :].bitcast(FP8X4),
                    scales=scales[:, c, :],
                    in_=grouped[:, c].rearrange("p w t -> p (w t)"),
                )
            return words, scales

        c_parts = const.tile([P, B, J_TILES, PASSES], F32)
        x_raw = {}
        x_grouped = {}
        x_words = {}

        def prepare_x(step):
            u, i = divmod(step, PIECES)
            width = EARLY_PIECE_COLS if u < EARLY_UNITS else PIECE_COLS
            if i == 0 and u + LOAD_AHEAD < UNITS:
                x_raw[u + LOAD_AHEAD] = load_unit(x_view(u + LOAD_AHEAD))
            if i == 0 and u < UNITS:
                x_grouped[u] = new_grouped()
                vector_regroups_rest(x_raw[u], x_grouped[u], width)
            if i == 1 and u - 1 not in x_words:
                x_words[u - 1] = quantise_unit(x_grouped[u - 1], x_pool, "x")
            if u < UNITS:
                scalar_regroups_piece(x_raw[u], x_grouped[u], i, width)

        y_rows = {}
        y_grouped = {}
        y_words = {}
        y_scales = {}

        def first_contraction_round(b, r):
            g, jt = divmod(r, UNIT_ROUNDS)
            words, scales = x_words[b * PASSES + g]
            if r == 0:
                y_rows[b] = y_pool.tile([P, J_TILES, N], BF16, name="y_rows", align_bytes=64)
                y_grouped[b] = y_pool.tile(
                    [P, PASSES, J, PACK], BF16, name="y_grouped", align_bytes=64
                )
                y_words[b] = y_pool.tile([P, PASSES, J], U32, name="y_words", align_bytes=64)
                y_scales[b] = y_pool.tile([P, PASSES, J], U8, name="y_scales", align_bytes=64)
            y_bank = psum.tile([P, J], F32, name="y_bank", bufs=Y_BANKS)
            cols = slice(jt * P, (jt + 1) * P)
            for c in range(PASSES):
                nc.tensor.matmul_mx(
                    out=y_bank[:],
                    lhsT=wj_words[:, c, cols].bitcast(FP8X4),
                    lhsT_scale=wj_scales[:, c, cols],
                    rhs=words[:, c, :].bitcast(FP8X4),
                    rhs_scale=scales[:, c, :],
                    start=(c == 0),
                    stop=(c == PASSES - 1),
                )
            nc.scalar.activation(
                out=y_rows[b][:, jt, g * J : (g + 1) * J], in_=y_bank[:], func=ACT.Identity,
                accum_out=c_parts[:, b, jt, g : g + 1],
            )

        def turn_round(b, k):
            g, pair = divmod(k, PAIRS)
            turned = psum.tile([P, 2, 2, P], F32, name="turned", bufs=TURN_BANKS)
            for i in range(2):
                jt = 2 * pair + i
                row_words = y_rows[b][:, jt, :].bitcast(F32)
                for u in range(2):
                    start = g * (J // 2) + u * P
                    nc.tensor.transpose(
                        turned[:, i, u, :], row_words[:, start : start + P], identity[:]
                    )
            cols = slice(2 * pair * P, 2 * (pair + 1) * P)
            out = y_grouped[b][:, g, cols, :].rearrange("p j t -> p (j t)").bitcast(F32)
            copy = nc.vector.tensor_copy if k in VECTOR_TURNS else nc.scalar.copy
            copy(
                out=out.rearrange("p (i j u) -> p i j u", i=2, u=2),
                in_=turned[:].rearrange("p i u j -> p i j u"),
            )

        def quantise_y(b, g):
            nc.vector.quantize_mx(
                out=y_words[b][:, g, :].bitcast(FP8X4),
                scales=y_scales[b][:, g, :],
                in_=y_grouped[b][:, g].rearrange("p j t -> p (j t)"),
            )

        c_columns = const.tile([P, P // J_TILES, J_TILES], F32)
        nc.vector.memset(c_columns[:], 0.0)

        def mean_of_items(columns, name):
            sums = psum.tile([P, B * J_TILES], F32, name="sums", tag="turned", bufs=TURN_BANKS)
            nc.tensor.matmul(
                out=sums[:], lhsT=one_over_j[:], rhs=columns.rearrange("p b t -> p (b t)"),
                start=True, stop=True,
            )
            mean = const.tile([P, B], F32, name=name)
            nc.vector.reduce_sum(
                out=mean[:], in_=sums[:].rearrange("p (b t) -> p b t", t=J_TILES), axis=AXIS.X
            )
            return mean

        def spread_over_tiles(values):
            return values[:].unsqueeze(2).to_broadcast([P, B, J_TILES])

        def write_p_sum():
            used = c_columns[:, :B, :]
            nc.vector.reduce_sum(out=used, in_=c_parts[:], axis=AXIS.X)
            mean = mean_of_items(used, "c_mean")
            nc.vector.tensor_sub(out=used, in0=used, in1=spread_over_tiles(mean))
            squares = const.tile([P, B, J_TILES], F32)
            nc.vector.tensor_mul(out=squares[:], in0=used, in1=used)
            variance = mean_of_items(squares[:], "c_variance")
            std = const.tile([P, B], F32, name="c_std")
            nc.scalar.activation(
                out=std[:], in_=variance[:], func=ACT.Sqrt, scale=J / (J - 1.0)
            )
            padded = const.tile([P, B], F32, name="c_padded")
            nc.vector.tensor_scalar_add(out=padded[:], in0=std[:], scalar1=EPS)
            inverse = const.tile([P, B], F32, name="c_inverse")
            nc.vector.reciprocal(out=inverse[:], in_=padded[:])
            nc.vector.tensor_mul(out=used, in0=used, in1=spread_over_tiles(inverse))
            rows = psum.tile([P, P], F32, name="rows", tag="turned", bufs=TURN_BANKS)
            nc.tensor.transpose(rows[:], c_columns[:].rearrange("p b t -> p (b t)"), identity[:])
            p_sum = const.tile([B * J_TILES, P], F32)
            nc.vector.tensor_mul(out=p_sum[:], in0=rows[: B * J_TILES, :], in1=gain_rows[:])
            nc.vector.tensor_add(out=p_sum[:], in0=p_sum[:], in1=bias_plus_one[:])
            nc.sync.dma_start(out=out_1.rearrange("b (t j) -> (b t) j", j=P), in_=p_sum[:])

        z_banks = {}
        z_mean_var = {}
        z_whole = {}
        z_padded = {}
        z_inverse = {}
        centred = {}
        normal = {}

        def second_contraction(b):
            six = stats.tile([P, J_TILES, 6], F32, name="z_six")
            for it in range(J_TILES):
                z_banks[b, it] = psum.tile([P, J], F32, name="z_bank", bufs=J_TILES)
                cols = slice(it * P, (it + 1) * P)
                for g in range(PASSES):
                    nc.tensor.matmul_mx(
                        out=z_banks[b, it][:],
                        lhsT=wi_words[:, g, cols].bitcast(FP8X4),
                        lhsT_scale=wi_scales[:, g, cols],
                        rhs=y_words[b][:, g, :].bitcast(FP8X4),
                        rhs_scale=y_scales[b][:, g, :],
                        start=(g == 0),
                        stop=(g == PASSES - 1),
                    )
                nc.vector.bn_stats(out=six[:, it, :], in_=z_banks[b, it][:])
            z_mean_var[b] = stats.tile([P, 2], F32, name="z_mean_var")
            nc.vector.bn_aggr(out=z_mean_var[b][:], in_=six[:].rearrange("p a s -> p (a s)"))

        def whole_statistics(b):
            averages = psum.tile([P, 3], F32, name="averages", tag="turned", bufs=TURN_BANKS)
            nc.tensor.matmul(
                out=averages[:, 0:2], lhsT=one_over_p[:], rhs=z_mean_var[b][:], start=True, stop=True
            )
            z_whole[b] = stats.tile([P, 2], F32, name="whole")
            nc.scalar.copy(out=z_whole[b][:], in_=averages[:, 0:2])
            distance = stats.tile([P, 1], F32, name="distance")
            nc.scalar.activation(
                out=distance[:], in_=z_mean_var[b][:, 0:1], func=ACT.Square,
                scale=-1.0, bias=z_whole[b][:, 0:1],
            )
            nc.tensor.matmul(
                out=averages[:, 2:3], lhsT=one_over_p[:], rhs=distance[:], start=True, stop=True
            )
            std = stats.tile([P, 1], F32, name="z_std")
            nc.scalar.activation(
                out=std[:], in_=averages[:, 2:3], func=ACT.Sqrt, bias=z_whole[b][:, 1:2]
            )
            z_padded[b] = stats.tile([P, 1], F32, name="z_padded")
            nc.scalar.activation(
                out=z_padded[b][:], in_=std[:], func=ACT.Identity,
                scale=math.sqrt(J * J / (J * J - 1.0)), bias=EPS,
            )

        def centre_z(b):
            centred[b] = result.tile([P, J_TILES, J], F32, name="centred")
            for it in range(J_TILES):
                nc.vector.scalar_tensor_tensor(
                    out=centred[b][:, it, :], in0=z_banks[b, it][:], scalar=z_whole[b][:, 0:1],
                    in1=gain[:, it, :], op0=ALU.subtract, op1=ALU.mult,
                )
            z_inverse[b] = stats.tile([P, 1], F32, name="z_inverse")
            nc.vector.reciprocal(out=z_inverse[b][:], in_=z_padded[b][:])
            normal[b] = result.tile([P, J_TILES, J], F32, name="normal")

        def write_out(b, first, count):
            tiles = slice(first, first + count)
            nc.vector.scalar_tensor_tensor(
                out=normal[b][:, tiles, :], in0=centred[b][:, tiles, :],
                scalar=z_inverse[b][:, 0:1], in1=bias[:, tiles, :], op0=ALU.mult, op1=ALU.add,
            )
            nc.sync.dma_start(
                out=out_0[b, first * P : (first + count) * P, :].rearrange("(a p) j -> p a j", p=P),
                in_=normal[b][:, tiles, :],
            )

        def finish_item(b, r):
            if r == 0 and b == 0:
                nc.vector.tensor_scalar_add(out=bias_plus_one[:], in0=bias_rows[:], scalar1=1.0)
            if r == 0 + Z_ROUND:
                second_contraction(b)
            if r == 1 + Z_ROUND:
                whole_statistics(b)
            if r == 2 + Z_ROUND:
                centre_z(b)
            if r == 3 + Z_ROUND or r == 4 + Z_ROUND:
                pair = 2 * (r - 3 - Z_ROUND)
                if b == B - 1:
                    write_out(b, pair, 1)
                    write_out(b, pair + 1, 1)
                elif pair == 0:
                    write_out(b, 0, J_TILES)
            if r == P_SUM_ROUND and b == B - 1:
                write_p_sum()

        x_raw[0] = load_unit(x_view(0))
        wj_raw = load_unit(permuted_xj_y.rearrange("(c p t) j -> p c t j", c=PASSES, t=PACK))
        for u in range(1, 1 + LOAD_AHEAD):
            x_raw[u] = load_unit(x_view(u))
        x_words[0] = prepare_unit_by_passes(x_raw[0], x_pool, "x")
        wj_words, wj_scales = prepare_unit_by_passes(wj_raw, const, "wj")
        wi_raw = raw_pool.tile([P, PASSES, PACK, J], BF16, name="raw")
        wi_view = permuted_xi_y.rearrange("(g u p e) i -> p g u (e i)", g=PASSES, u=2, e=2)
        for g in range(PASSES):
            nc.sync.dma_start(
                out=wi_raw[:, g].rearrange("p (u e) i -> p u (e i)", e=2), in_=wi_view[:, g]
            )
        for step in range(PIECES, AHEAD):
            prepare_x(step)

        gain = const.tile([P, J_TILES, J], BF16)
        bias = const.tile([P, J_TILES, J], BF16)
        gain_rows = const.tile([B * J_TILES, P], BF16)
        bias_rows = const.tile([B * J_TILES, P], BF16)
        bias_plus_one = const.tile([B * J_TILES, P], F32)

        def load_gains():
            nc.sync.dma_start(out=gain[:], in_=gamma_p.rearrange("(a p) j -> p a j", p=P))
            nc.sync.dma_start(out=bias[:], in_=beta_p.rearrange("(a p) j -> p a j", p=P))
            for item in range(B):
                rows = slice(item * J_TILES, (item + 1) * J_TILES)
                nc.sync.dma_start(
                    out=gain_rows[rows, :], in_=gamma_p_sum.rearrange("(t j) -> t j", j=P)
                )
                nc.sync.dma_start(
                    out=bias_rows[rows, :], in_=beta_p_sum.rearrange("(t j) -> t j", j=P)
                )

        for b in range(B + 1):
            for r in range(ROUNDS):
                turn = b * ROUNDS + r - 1 - TURN_LAG
                if turn % 2 == 0 and 0 <= turn // 2 < UNITS * PAIRS:
                    item, k = divmod(turn // 2, PASSES * PAIRS)
                    turn_round(item, k)
                    if k % PAIRS == PAIRS - 1:
                        quantise_y(item, k // PAIRS)
                if b < B:
                    step = b * ROUNDS + r + AHEAD
                    if step <= UNITS * PIECES + 1:
                        prepare_x(step)
                    first_contraction_round(b, r)
                if b == 0 and r == WI_ROUND:
                    wi_grouped = new_grouped()
                    vector_regroups_rest(wi_raw, wi_grouped, EARLY_PIECE_COLS)
                    for i in range(PIECES):
                        scalar_regroups_piece(wi_raw, wi_grouped, i, EARLY_PIECE_COLS)
                    wi_words, wi_scales = quantise_unit(wi_grouped, const, "wi")
                if b * ROUNDS + r == GAIN_ROUND:
                    load_gains()
                if b > 0:
                    finish_item(b - 1, r)
